import numpy as np
import ml_dtypes

BF16 = ml_dtypes.bfloat16


def bf(x):
    return np.asarray(x, np.float32).astype(BF16)


def f32(x):
    return np.asarray(x, np.float32)


def f64(x):
    return np.asarray(x).astype(np.float64)


def striped(idx):
    return np.tile(idx.reshape(-1, 16).T, (8, 1))


C, S, K, N = 256, 1024, 4, 4096
GAMMA, XI, SPAN = -0.1, 1.1, 5.0


def soft_mask(v):
    return np.clip((XI - GAMMA) / (1.0 + np.exp(-v)) + GAMMA, 0.0, 1.0)


def setup_inputs():
    return {"weight": f32(np.random.standard_normal((C, S))), "sparse_mask": f32(np.random.uniform(-SPAN, SPAN, (C, S))), "scales": f32(np.random.standard_normal((1, N)) / np.sqrt(K)), "row_scale": f32(np.random.standard_normal((C, 1))), "offs": striped(np.concatenate([np.random.permutation(S) for _ in range(K)]))}


def reference(weight, sparse_mask, scales, row_scale, offs):
    idx = offs[:16].T.reshape(-1)
    sw = f64(weight) * soft_mask(f64(sparse_mask))
    term = sw[:, idx] * f64(scales)
    return f64(row_scale) * term.reshape(C, K, S).sum(axis=1)

@@ -1,0 +1,80 @@
+import concourse.mybir as mybir
+from concourse.masks import make_identity
+
+F32 = mybir.dt.float32
+U16 = mybir.dt.uint16
+ACT = mybir.ActivationFunctionType
+ALU = mybir.AluOpType
+
+P = 128
+C, S, K = 256, 1024, 4
+N = K * S
+BLOCKS = C // P
+BANK = 512
+HALVES = S // BANK
+
+FLOPS = 2 * C * N
+
+
+def tile_permutatedsoftsparse_kernel(tc, weight, sparse_mask, scales, row_scale, offs, out):
+    nc = tc.nc
+    with (
+        tc.tile_pool(name="held", bufs=1) as held,
+        tc.tile_pool(name="terms", bufs=4) as terms,
+        tc.psum_pool(name="sums", bufs=1) as sums,
+    ):
+        offsets = held.tile([P, N // 16], U16, name="offsets")
+        nc.sync.dma_start(offsets[:], offs)
+
+        logits = [held.tile([P, S], F32, name=f"logits{b}") for b in range(BLOCKS)]
+        dense = [held.tile([P, S], F32, name=f"dense{b}") for b in range(BLOCKS)]
+        row_gain = [held.tile([P, 1], F32, name=f"row_gain{b}") for b in range(BLOCKS)]
+        scales_all = held.tile([P, N], F32, name="scales_all")
+
+        def load_block(b):
+            rows = slice(b * P, (b + 1) * P)
+            nc.sync.dma_start(logits[b][:], sparse_mask[rows, :])
+            nc.scalar.dma_start(dense[b][:], weight[rows, :])
+
+        def load_scales(queue, k):
+            cols = slice(k * S, (k + 1) * S)
+            queue.dma_start(scales_all[:, cols], scales[0, cols].partition_broadcast(P))
+
+        load_block(0)
+        load_scales(nc.sync, 0)
+        load_scales(nc.scalar, 1)
+        load_block(1)
+        load_scales(nc.sync, 2)
+        load_scales(nc.scalar, 3)
+        for b in range(BLOCKS):
+            nc.sync.dma_start(row_gain[b][:], row_scale[b * P : (b + 1) * P, :])
+
+        identity = held.tile([P, P], F32, name="identity")
+        make_identity(nc, identity[:])
+
+        for b in range(BLOCKS):
+            gate = held.tile([P, S], F32, name=f"gate{b}")
+            nc.scalar.activation(gate[:], logits[b][:], ACT.Sigmoid)
+            nc.scalar.activation(gate[:], gate[:], ACT.Relu, bias=-0.1, scale=1.2)
+            sw = held.tile([P, S], F32, name=f"sw{b}")
+            nc.vector.scalar_tensor_tensor(sw[:], gate[:], 1.0, dense[b][:], ALU.min, ALU.mult)
+
+            total = [sums.tile([P, BANK], F32, name=f"total{b}_{h}") for h in range(HALVES)]
+            for k in range(K):
+                term = terms.tile([P, S], F32, name="term")
+                nc.vector.tensor_tensor(
+                    term[:],
+                    sw[:].indirect(offsets[:, k * (S // 16) : (k + 1) * (S // 16)]),
+                    scales_all[:, k * S : (k + 1) * S],
+                    ALU.mult,
+                )
+                for h in range(HALVES):
+                    nc.tensor.matmul(
+                        total[h][:], identity[:], term[:, h * BANK : (h + 1) * BANK], start=(k == 0), stop=(k == K - 1)
+                    )
+
+            result = held.tile([P, S], F32, name=f"result{b}")
+            for h in range(HALVES):
+                cols = slice(h * BANK, (h + 1) * BANK)
+                nc.scalar.activation(result[:, cols], total[h][:], ACT.Identity, scale=row_gain[b][:, 0:1])
+                nc.sync.dma_start(out[b * P : (b + 1) * P, cols], result[:, cols])

@@ -10,8 +10,8 @@ P = 128
 C, S, K = 256, 1024, 4
 N = K * S
 BLOCKS = C // P
-BANK = 512
-HALVES = S // BANK
+HALF = 512
+HALVES = S // HALF
 
 FLOPS = 2 * C * N
 
@@ -24,28 +24,28 @@ def tile_permutatedsoftsparse_kernel(tc, weight, sparse_mask, scales, row_scale,
         tc.psum_pool(name="sums", bufs=1) as sums,
     ):
         offsets = held.tile([P, N // 16], U16, name="offsets")
-        nc.sync.dma_start(offsets[:], offs)
-
         logits = [held.tile([P, S], F32, name=f"logits{b}") for b in range(BLOCKS)]
         dense = [held.tile([P, S], F32, name=f"dense{b}") for b in range(BLOCKS)]
         row_gain = [held.tile([P, 1], F32, name=f"row_gain{b}") for b in range(BLOCKS)]
         scales_all = held.tile([P, N], F32, name="scales_all")
 
-        def load_block(b):
-            rows = slice(b * P, (b + 1) * P)
-            nc.sync.dma_start(logits[b][:], sparse_mask[rows, :])
-            nc.scalar.dma_start(dense[b][:], weight[rows, :])
+        def load_halves(tile, source, b):
+            for h, queue in enumerate((nc.sync, nc.scalar)):
+                cols = slice(h * HALF, (h + 1) * HALF)
+                queue.dma_start(tile[:, cols], source[b * P : (b + 1) * P, cols])
 
-        def load_scales(queue, k):
-            cols = slice(k * S, (k + 1) * S)
-            queue.dma_start(scales_all[:, cols], scales[0, cols].partition_broadcast(P))
+        def load_scales(h):
+            for k in range(K):
+                cols = slice(k * S + h * HALF, k * S + (h + 1) * HALF)
+                nc.sync.dma_start(scales_all[:, cols], scales[0, cols].partition_broadcast(P))
 
-        load_block(0)
-        load_scales(nc.sync, 0)
-        load_scales(nc.scalar, 1)
-        load_block(1)
-        load_scales(nc.sync, 2)
-        load_scales(nc.scalar, 3)
+        load_halves(logits[0], sparse_mask, 0)
+        load_halves(dense[0], weight, 0)
+        nc.sync.dma_start(offsets[:], offs)
+        load_scales(0)
+        load_halves(logits[1], sparse_mask, 1)
+        load_scales(1)
+        load_halves(dense[1], weight, 1)
         for b in range(BLOCKS):
             nc.sync.dma_start(row_gain[b][:], row_scale[b * P : (b + 1) * P, :])
 
@@ -54,27 +54,25 @@ def tile_permutatedsoftsparse_kernel(tc, weight, sparse_mask, scales, row_scale,
 
         for b in range(BLOCKS):
             gate = held.tile([P, S], F32, name=f"gate{b}")
-            nc.scalar.activation(gate[:], logits[b][:], ACT.Sigmoid)
-            nc.scalar.activation(gate[:], gate[:], ACT.Relu, bias=-0.1, scale=1.2)
             sw = held.tile([P, S], F32, name=f"sw{b}")
-            nc.vector.scalar_tensor_tensor(sw[:], gate[:], 1.0, dense[b][:], ALU.min, ALU.mult)
-
-            total = [sums.tile([P, BANK], F32, name=f"total{b}_{h}") for h in range(HALVES)]
-            for k in range(K):
-                term = terms.tile([P, S], F32, name="term")
-                nc.vector.tensor_tensor(
-                    term[:],
-                    sw[:].indirect(offsets[:, k * (S // 16) : (k + 1) * (S // 16)]),
-                    scales_all[:, k * S : (k + 1) * S],
-                    ALU.mult,
-                )
-                for h in range(HALVES):
-                    nc.tensor.matmul(
-                        total[h][:], identity[:], term[:, h * BANK : (h + 1) * BANK], start=(k == 0), stop=(k == K - 1)
-                    )
-
-            result = held.tile([P, S], F32, name=f"result{b}")
             for h in range(HALVES):
-                cols = slice(h * BANK, (h + 1) * BANK)
-                nc.scalar.activation(result[:, cols], total[h][:], ACT.Identity, scale=row_gain[b][:, 0:1])
-                nc.sync.dma_start(out[b * P : (b + 1) * P, cols], result[:, cols])
+                cols = slice(h * HALF, (h + 1) * HALF)
+                nc.scalar.activation(gate[:, cols], logits[b][:, cols], ACT.Sigmoid)
+                nc.scalar.activation(gate[:, cols], gate[:, cols], ACT.Relu, bias=-0.1, scale=1.2)
+                nc.vector.scalar_tensor_tensor(sw[:, cols], gate[:, cols], 1.0, dense[b][:, cols], ALU.min, ALU.mult)
+
+            for h in range(HALVES):
+                total = sums.tile([P, HALF], F32, name=f"total{b}_{h}")
+                for k in range(K):
+                    first = k * S + h * HALF
+                    term = terms.tile([P, HALF], F32, name="term")
+                    nc.vector.tensor_tensor(
+                        term[:],
+                        sw[:].indirect(offsets[:, first // 16 : (first + HALF) // 16]),
+                        scales_all[:, first : first + HALF],
+                        ALU.mult,
+                    )
+                    nc.tensor.matmul(total[:], identity[:], term[:], start=(k == 0), stop=(k == K - 1))
+                result = held.tile([P, HALF], F32, name=f"result{b}_{h}")
+                nc.scalar.activation(result[:], total[:], ACT.Identity, scale=row_gain[b][:, 0:1])
+                nc.sync.dma_start(out[b * P : (b + 1) * P, h * HALF : (h + 1) * HALF], result[:])

@@ -12,6 +12,8 @@ N = K * S
 BLOCKS = C // P
 HALF = 512
 HALVES = S // HALF
+CHUNK = 256
+WIDTHS = ((HALF, HALF), (HALF, HALF // 2, HALF // 2))
 
 FLOPS = 2 * C * N
 
@@ -29,50 +31,56 @@ def tile_permutatedsoftsparse_kernel(tc, weight, sparse_mask, scales, row_scale,
         row_gain = [held.tile([P, 1], F32, name=f"row_gain{b}") for b in range(BLOCKS)]
         scales_all = held.tile([P, N], F32, name="scales_all")
 
-        def load_halves(tile, source, b):
-            for h, queue in enumerate((nc.sync, nc.scalar)):
-                cols = slice(h * HALF, (h + 1) * HALF)
-                queue.dma_start(tile[:, cols], source[b * P : (b + 1) * P, cols])
+        def load_chunks(tile, source, b):
+            for c in range(S // CHUNK):
+                cols = slice(c * CHUNK, (c + 1) * CHUNK)
+                nc.sync.dma_start(tile[:, cols], source[b * P : (b + 1) * P, cols])
 
         def load_scales(h):
             for k in range(K):
                 cols = slice(k * S + h * HALF, k * S + (h + 1) * HALF)
                 nc.sync.dma_start(scales_all[:, cols], scales[0, cols].partition_broadcast(P))
 
-        load_halves(logits[0], sparse_mask, 0)
-        load_halves(dense[0], weight, 0)
+        load_chunks(logits[0], sparse_mask, 0)
+        load_chunks(dense[0], weight, 0)
         nc.sync.dma_start(offsets[:], offs)
         load_scales(0)
-        load_halves(logits[1], sparse_mask, 1)
+        load_chunks(logits[1], sparse_mask, 1)
         load_scales(1)
-        load_halves(dense[1], weight, 1)
+        load_chunks(dense[1], weight, 1)
         for b in range(BLOCKS):
             nc.sync.dma_start(row_gain[b][:], row_scale[b * P : (b + 1) * P, :])
 
         identity = held.tile([P, P], F32, name="identity")
         make_identity(nc, identity[:])
 
+        warm_up = sums.tile([P, CHUNK], F32, name="warm_up")
+        for c in range(S // CHUNK):
+            nc.tensor.matmul(warm_up[:], identity[:], logits[0][:, c * CHUNK : (c + 1) * CHUNK], start=True, stop=True)
+
         for b in range(BLOCKS):
             gate = held.tile([P, S], F32, name=f"gate{b}")
             sw = held.tile([P, S], F32, name=f"sw{b}")
-            for h in range(HALVES):
-                cols = slice(h * HALF, (h + 1) * HALF)
+            for c in range(S // CHUNK):
+                cols = slice(c * CHUNK, (c + 1) * CHUNK)
                 nc.scalar.activation(gate[:, cols], logits[b][:, cols], ACT.Sigmoid)
                 nc.scalar.activation(gate[:, cols], gate[:, cols], ACT.Relu, bias=-0.1, scale=1.2)
                 nc.vector.scalar_tensor_tensor(sw[:, cols], gate[:, cols], 1.0, dense[b][:, cols], ALU.min, ALU.mult)
 
-            for h in range(HALVES):
-                total = sums.tile([P, HALF], F32, name=f"total{b}_{h}")
+            start = 0
+            for width in WIDTHS[b]:
+                total = sums.tile([P, width], F32, name=f"total{b}_{start}")
                 for k in range(K):
-                    first = k * S + h * HALF
-                    term = terms.tile([P, HALF], F32, name="term")
+                    first = k * S + start
+                    term = terms.tile([P, width], F32, name="term")
                     nc.vector.tensor_tensor(
                         term[:],
-                        sw[:].indirect(offsets[:, first // 16 : (first + HALF) // 16]),
-                        scales_all[:, first : first + HALF],
+                        sw[:].indirect(offsets[:, first // 16 : (first + width) // 16]),
+                        scales_all[:, first : first + width],
                         ALU.mult,
                     )
                     nc.tensor.matmul(total[:], identity[:], term[:], start=(k == 0), stop=(k == K - 1))
-                result = held.tile([P, HALF], F32, name=f"result{b}_{h}")
+                result = held.tile([P, width], F32, name=f"result{b}_{start}")
                 nc.scalar.activation(result[:], total[:], ACT.Identity, scale=row_gain[b][:, 0:1])
-                nc.sync.dma_start(out[b * P : (b + 1) * P, h * HALF : (h + 1) * HALF], result[:])
+                nc.sync.dma_start(out[b * P : (b + 1) * P, start : start + width], result[:])
+                start += width

@@ -54,10 +54,6 @@ def tile_permutatedsoftsparse_kernel(tc, weight, sparse_mask, scales, row_scale,
         identity = held.tile([P, P], F32, name="identity")
         make_identity(nc, identity[:])
 
-        warm_up = sums.tile([P, CHUNK], F32, name="warm_up")
-        for c in range(S // CHUNK):
-            nc.tensor.matmul(warm_up[:], identity[:], logits[0][:, c * CHUNK : (c + 1) * CHUNK], start=True, stop=True)
-
         for b in range(BLOCKS):
             gate = held.tile([P, S], F32, name=f"gate{b}")
             sw = held.tile([P, S], F32, name=f"sw{b}")

@@ -13,7 +13,7 @@ BLOCKS = C // P
 HALF = 512
 HALVES = S // HALF
 CHUNK = 256
-WIDTHS = ((HALF, HALF), (HALF, HALF // 2, HALF // 2))
+LAST = HALF // 2
 
 FLOPS = 2 * C * N
 
@@ -54,7 +54,7 @@ def tile_permutatedsoftsparse_kernel(tc, weight, sparse_mask, scales, row_scale,
         identity = held.tile([P, P], F32, name="identity")
         make_identity(nc, identity[:])
 
-        for b in range(BLOCKS):
+        def make_sw(b):
             gate = held.tile([P, S], F32, name=f"gate{b}")
             sw = held.tile([P, S], F32, name=f"sw{b}")
             for c in range(S // CHUNK):
@@ -62,21 +62,42 @@ def tile_permutatedsoftsparse_kernel(tc, weight, sparse_mask, scales, row_scale,
                 nc.scalar.activation(gate[:, cols], logits[b][:, cols], ACT.Sigmoid)
                 nc.scalar.activation(gate[:, cols], gate[:, cols], ACT.Relu, bias=-0.1, scale=1.2)
                 nc.vector.scalar_tensor_tensor(sw[:, cols], gate[:, cols], 1.0, dense[b][:, cols], ALU.min, ALU.mult)
+            return sw
 
-            start = 0
-            for width in WIDTHS[b]:
-                total = sums.tile([P, width], F32, name=f"total{b}_{start}")
-                for k in range(K):
-                    first = k * S + start
-                    term = terms.tile([P, width], F32, name="term")
-                    nc.vector.tensor_tensor(
-                        term[:],
-                        sw[:].indirect(offsets[:, first // 16 : (first + width) // 16]),
-                        scales_all[:, first : first + width],
-                        ALU.mult,
-                    )
-                    nc.tensor.matmul(total[:], identity[:], term[:], start=(k == 0), stop=(k == K - 1))
-                result = held.tile([P, width], F32, name=f"result{b}_{start}")
-                nc.scalar.activation(result[:], total[:], ACT.Identity, scale=row_gain[b][:, 0:1])
-                nc.sync.dma_start(out[b * P : (b + 1) * P, start : start + width], result[:])
-                start += width
+        def gather_term(sw, k, start, width):
+            first = k * S + start
+            term = terms.tile([P, width], F32, name="term")
+            nc.vector.tensor_tensor(
+                term[:],
+                sw[:].indirect(offsets[:, first // 16 : (first + width) // 16]),
+                scales_all[:, first : first + width],
+                ALU.mult,
+            )
+            return term
+
+        def scaled_sum(b, sw, ks, start, width):
+            total = sums.tile([P, width], F32, name=f"total{b}_{start}")
+            for k in ks:
+                term = gather_term(sw, k, start, width)
+                nc.tensor.matmul(total[:], identity[:], term[:], start=(k == ks[0]), stop=(k == ks[-1]))
+            scaled = held.tile([P, width], F32, name=f"scaled{b}_{start}")
+            nc.scalar.activation(scaled[:], total[:], ACT.Identity, scale=row_gain[b][:, 0:1])
+            return scaled
+
+        def store(b, start, width, result):
+            nc.sync.dma_start(out[b * P : (b + 1) * P, start : start + width], result[:])
+
+        every_k = list(range(K))
+
+        sw = make_sw(0)
+        for start in range(0, S, HALF):
+            store(0, start, HALF, scaled_sum(0, sw, every_k, start, HALF))
+
+        sw = make_sw(1)
+        store(1, 0, HALF, scaled_sum(1, sw, every_k, 0, HALF))
+        others = scaled_sum(1, sw, every_k[:-1], S - LAST, LAST)
+        store(1, HALF, LAST, scaled_sum(1, sw, every_k, HALF, LAST))
+        term = gather_term(sw, K - 1, S - LAST, LAST)
+        result = held.tile([P, LAST], F32, name="result")
+        nc.vector.scalar_tensor_tensor(result[:], term[:], row_gain[1][:, 0:1], others[:], ALU.mult, ALU.add)
+        store(1, S - LAST, LAST, result)

@@ -54,13 +54,18 @@ def tile_permutatedsoftsparse_kernel(tc, weight, sparse_mask, scales, row_scale,
         identity = held.tile([P, P], F32, name="identity")
         make_identity(nc, identity[:])
 
-        def make_sw(b):
+        def make_sw(b, chunks_clamped_by_vector):
             gate = held.tile([P, S], F32, name=f"gate{b}")
             sw = held.tile([P, S], F32, name=f"sw{b}")
-            for c in range(S // CHUNK):
-                cols = slice(c * CHUNK, (c + 1) * CHUNK)
+            chunks = [slice(c * CHUNK, (c + 1) * CHUNK) for c in range(S // CHUNK)]
+            for c, cols in enumerate(chunks):
                 nc.scalar.activation(gate[:, cols], logits[b][:, cols], ACT.Sigmoid)
-                nc.scalar.activation(gate[:, cols], gate[:, cols], ACT.Relu, bias=-0.1, scale=1.2)
+                if c < chunks_clamped_by_vector:
+                    nc.vector.tensor_scalar(gate[:, cols], gate[:, cols], 1.2, -0.1, ALU.mult, ALU.add)
+                    nc.vector.tensor_scalar_max(gate[:, cols], gate[:, cols], 0.0)
+                else:
+                    nc.scalar.activation(gate[:, cols], gate[:, cols], ACT.Relu, bias=-0.1, scale=1.2)
+            for cols in chunks:
                 nc.vector.scalar_tensor_tensor(sw[:, cols], gate[:, cols], 1.0, dense[b][:, cols], ALU.min, ALU.mult)
             return sw
 
@@ -89,11 +94,11 @@ def tile_permutatedsoftsparse_kernel(tc, weight, sparse_mask, scales, row_scale,
 
         every_k = list(range(K))
 
-        sw = make_sw(0)
+        sw = make_sw(0, S // CHUNK // 2)
         for start in range(0, S, HALF):
             store(0, start, HALF, scaled_sum(0, sw, every_k, start, HALF))
 
-        sw = make_sw(1)
+        sw = make_sw(1, 0)
         store(1, 0, HALF, scaled_sum(1, sw, every_k, 0, HALF))
         others = scaled_sum(1, sw, every_k[:-1], S - LAST, LAST)
         store(1, HALF, LAST, scaled_sum(1, sw, every_k, HALF, LAST))

@@ -94,7 +94,7 @@ def tile_permutatedsoftsparse_kernel(tc, weight, sparse_mask, scales, row_scale,
 
         every_k = list(range(K))
 
-        sw = make_sw(0, S // CHUNK // 2)
+        sw = make_sw(0, S // CHUNK - 1)
         for start in range(0, S, HALF):
             store(0, start, HALF, scaled_sum(0, sw, every_k, start, HALF))
 

@@ -36,18 +36,19 @@ def tile_permutatedsoftsparse_kernel(tc, weight, sparse_mask, scales, row_scale,
                 cols = slice(c * CHUNK, (c + 1) * CHUNK)
                 nc.sync.dma_start(tile[:, cols], source[b * P : (b + 1) * P, cols])
 
-        def load_scales(h):
-            for k in range(K):
+        def load_scales(h, ks):
+            for k in ks:
                 cols = slice(k * S + h * HALF, k * S + (h + 1) * HALF)
                 nc.sync.dma_start(scales_all[:, cols], scales[0, cols].partition_broadcast(P))
 
         load_chunks(logits[0], sparse_mask, 0)
         load_chunks(dense[0], weight, 0)
         nc.sync.dma_start(offsets[:], offs)
-        load_scales(0)
+        load_scales(0, range(K))
         load_chunks(logits[1], sparse_mask, 1)
-        load_scales(1)
+        load_scales(1, range(K - 1))
         load_chunks(dense[1], weight, 1)
+        load_scales(1, [K - 1])
         for b in range(BLOCKS):
             nc.sync.dma_start(row_gain[b][:], row_scale[b * P : (b + 1) * P, :])
 

@@ -28,12 +28,12 @@ def tile_permutatedsoftsparse_kernel(tc, weight, sparse_mask, scales, row_scale,
         offsets = held.tile([P, N // 16], U16, name="offsets")
         logits = [held.tile([P, S], F32, name=f"logits{b}") for b in range(BLOCKS)]
         dense = [held.tile([P, S], F32, name=f"dense{b}") for b in range(BLOCKS)]
-        row_gain = [held.tile([P, 1], F32, name=f"row_gain{b}") for b in range(BLOCKS)]
+        row_gain = held.tile([P, BLOCKS], F32, name="row_gain")
         scales_all = held.tile([P, N], F32, name="scales_all")
 
-        def load_chunks(tile, source, b):
-            for c in range(S // CHUNK):
-                cols = slice(c * CHUNK, (c + 1) * CHUNK)
+        def load_rows(tile, source, b, width):
+            for start in range(0, S, width):
+                cols = slice(start, start + width)
                 nc.sync.dma_start(tile[:, cols], source[b * P : (b + 1) * P, cols])
 
         def load_scales(h, ks):
@@ -41,16 +41,15 @@ def tile_permutatedsoftsparse_kernel(tc, weight, sparse_mask, scales, row_scale,
                 cols = slice(k * S + h * HALF, k * S + (h + 1) * HALF)
                 nc.sync.dma_start(scales_all[:, cols], scales[0, cols].partition_broadcast(P))
 
-        load_chunks(logits[0], sparse_mask, 0)
-        load_chunks(dense[0], weight, 0)
+        load_rows(logits[0], sparse_mask, 0, CHUNK)
+        load_rows(dense[0], weight, 0, CHUNK)
         nc.sync.dma_start(offsets[:], offs)
         load_scales(0, range(K))
-        load_chunks(logits[1], sparse_mask, 1)
+        load_rows(logits[1], sparse_mask, 1, S)
         load_scales(1, range(K - 1))
-        load_chunks(dense[1], weight, 1)
+        load_rows(dense[1], weight, 1, S)
         load_scales(1, [K - 1])
-        for b in range(BLOCKS):
-            nc.sync.dma_start(row_gain[b][:], row_scale[b * P : (b + 1) * P, :])
+        nc.sync.dma_start(row_gain[:], row_scale.rearrange("(b p) o -> p (b o)", p=P))
 
         identity = held.tile([P, P], F32, name="identity")
         make_identity(nc, identity[:])
@@ -81,14 +80,14 @@ def tile_permutatedsoftsparse_kernel(tc, weight, sparse_mask, scales, row_scale,
             )
             return term
 
-        def scaled_sum(b, sw, ks, start, width):
+        def scaled_sum(b, sw, ks, start, width, scaled, before_last=None):
             total = sums.tile([P, width], F32, name=f"total{b}_{start}")
             for k in ks:
+                made = before_last() if before_last is not None and k == ks[-1] else None
                 term = gather_term(sw, k, start, width)
                 nc.tensor.matmul(total[:], identity[:], term[:], start=(k == ks[0]), stop=(k == ks[-1]))
-            scaled = held.tile([P, width], F32, name=f"scaled{b}_{start}")
-            nc.scalar.activation(scaled[:], total[:], ACT.Identity, scale=row_gain[b][:, 0:1])
-            return scaled
+            nc.scalar.activation(scaled, total[:], ACT.Identity, scale=row_gain[:, b : b + 1])
+            return made
 
         def store(b, start, width, result):
             nc.sync.dma_start(out[b * P : (b + 1) * P, start : start + width], result[:])
@@ -96,14 +95,20 @@ def tile_permutatedsoftsparse_kernel(tc, weight, sparse_mask, scales, row_scale,
         every_k = list(range(K))
 
         sw = make_sw(0, S // CHUNK - 1)
-        for start in range(0, S, HALF):
-            store(0, start, HALF, scaled_sum(0, sw, every_k, start, HALF))
+        scaled = held.tile([P, S], F32, name="scaled0")
+        scaled_sum(0, sw, every_k, 0, HALF, scaled[:, 0:HALF])
+        sw = scaled_sum(0, sw, every_k, HALF, HALF, scaled[:, HALF:S], before_last=lambda: make_sw(1, 0))
+        store(0, 0, S, scaled)
 
-        sw = make_sw(1, 0)
-        store(1, 0, HALF, scaled_sum(1, sw, every_k, 0, HALF))
-        others = scaled_sum(1, sw, every_k[:-1], S - LAST, LAST)
-        store(1, HALF, LAST, scaled_sum(1, sw, every_k, HALF, LAST))
+        left = held.tile([P, HALF], F32, name="left")
+        scaled_sum(1, sw, every_k, 0, HALF, left[:])
+        store(1, 0, HALF, left)
+        others = held.tile([P, LAST], F32, name="others")
+        scaled_sum(1, sw, every_k[:-1], S - LAST, LAST, others[:])
+        middle = held.tile([P, LAST], F32, name="middle")
+        scaled_sum(1, sw, every_k, HALF, LAST, middle[:])
+        store(1, HALF, LAST, middle)
         term = gather_term(sw, K - 1, S - LAST, LAST)
         result = held.tile([P, LAST], F32, name="result")
-        nc.vector.scalar_tensor_tensor(result[:], term[:], row_gain[1][:, 0:1], others[:], ALU.mult, ALU.add)
+        nc.vector.scalar_tensor_tensor(result[:], term[:], row_gain[:, 1:2], others[:], ALU.mult, ALU.add)
         store(1, S - LAST, LAST, result)

@@ -13,7 +13,7 @@ BLOCKS = C // P
 HALF = 512
 HALVES = S // HALF
 CHUNK = 256
-LAST = HALF // 2
+PIECE = HALF // 2
 
 FLOPS = 2 * C * N
 
@@ -69,15 +69,17 @@ def tile_permutatedsoftsparse_kernel(tc, weight, sparse_mask, scales, row_scale,
                 nc.vector.scalar_tensor_tensor(sw[:, cols], gate[:, cols], 1.0, dense[b][:, cols], ALU.min, ALU.mult)
             return sw
 
-        def gather_term(sw, k, start, width):
-            first = k * S + start
+        def gather_term(sw, k, start, width, pieces=1):
             term = terms.tile([P, width], F32, name="term")
-            nc.vector.tensor_tensor(
-                term[:],
-                sw[:].indirect(offsets[:, first // 16 : (first + width) // 16]),
-                scales_all[:, first : first + width],
-                ALU.mult,
-            )
+            step = width // pieces
+            for within in range(0, width, step):
+                first = k * S + start + within
+                nc.vector.tensor_tensor(
+                    term[:, within : within + step],
+                    sw[:].indirect(offsets[:, first // 16 : (first + step) // 16]),
+                    scales_all[:, first : first + step],
+                    ALU.mult,
+                )
             return term
 
         def scaled_sum(b, sw, ks, start, width, scaled, before_last=None):
@@ -103,12 +105,20 @@ def tile_permutatedsoftsparse_kernel(tc, weight, sparse_mask, scales, row_scale,
         left = held.tile([P, HALF], F32, name="left")
         scaled_sum(1, sw, every_k, 0, HALF, left[:])
         store(1, 0, HALF, left)
-        others = held.tile([P, LAST], F32, name="others")
-        scaled_sum(1, sw, every_k[:-1], S - LAST, LAST, others[:])
-        middle = held.tile([P, LAST], F32, name="middle")
-        scaled_sum(1, sw, every_k, HALF, LAST, middle[:])
-        store(1, HALF, LAST, middle)
-        term = gather_term(sw, K - 1, S - LAST, LAST)
-        result = held.tile([P, LAST], F32, name="result")
-        nc.vector.scalar_tensor_tensor(result[:], term[:], row_gain[:, 1:2], others[:], ALU.mult, ALU.add)
-        store(1, S - LAST, LAST, result)
+        diagonal = held.tile([P, P], F32, name="diagonal")
+        nc.scalar.activation(diagonal[:], identity[:], ACT.Identity, scale=row_gain[:, 1:2])
+        columns = [slice(start, start + PIECE) for start in range(0, HALF, PIECE)]
+        others = [sums.tile([P, PIECE], F32, name=f"others{cols.start}") for cols in columns]
+        for k in every_k[:-1]:
+            term = gather_term(sw, k, HALF, HALF, pieces=len(columns) if k == every_k[-2] else 1)
+            for cols, total in zip(columns, others):
+                nc.tensor.matmul(
+                    total[:], diagonal[:], term[:, cols], start=(k == every_k[0]), stop=(k == every_k[-2])
+                )
+        term = gather_term(sw, every_k[-1], HALF, HALF, pieces=len(columns))
+        for cols, total in zip(columns, others):
+            result = held.tile([P, PIECE], F32, name=f"result{cols.start}")
+            nc.vector.scalar_tensor_tensor(
+                result[:], term[:, cols], row_gain[:, 1:2], total[:], ALU.mult, ALU.add
+            )
+            store(1, HALF + cols.start, PIECE, result)

@@ -22,7 +22,7 @@ def tile_permutatedsoftsparse_kernel(tc, weight, sparse_mask, scales, row_scale,
     nc = tc.nc
     with (
         tc.tile_pool(name="held", bufs=1) as held,
-        tc.tile_pool(name="terms", bufs=4) as terms,
+        tc.tile_pool(name="terms", bufs=6) as terms,
         tc.psum_pool(name="sums", bufs=1) as sums,
     ):
         offsets = held.tile([P, N // 16], U16, name="offsets")

import concourse.mybir as mybir
from concourse.masks import make_identity

F32 = mybir.dt.float32
U16 = mybir.dt.uint16
ACT = mybir.ActivationFunctionType
ALU = mybir.AluOpType

P = 128
C, S, K = 256, 1024, 4
N = K * S
BLOCKS = C // P
HALF = 512
HALVES = S // HALF
CHUNK = 256
PIECE = HALF // 2

FLOPS = 2 * C * N


def tile_permutatedsoftsparse_kernel(tc, weight, sparse_mask, scales, row_scale, offs, out):
    nc = tc.nc
    with (
        tc.tile_pool(name="held", bufs=1) as held,
        tc.tile_pool(name="terms", bufs=6) as terms,
        tc.psum_pool(name="sums", bufs=1) as sums,
    ):
        offsets = held.tile([P, N // 16], U16, name="offsets")
        logits = [held.tile([P, S], F32, name=f"logits{b}") for b in range(BLOCKS)]
        dense = [held.tile([P, S], F32, name=f"dense{b}") for b in range(BLOCKS)]
        row_gain = held.tile([P, BLOCKS], F32, name="row_gain")
        scales_all = held.tile([P, N], F32, name="scales_all")

        def load_rows(tile, source, b, width):
            for start in range(0, S, width):
                cols = slice(start, start + width)
                nc.sync.dma_start(tile[:, cols], source[b * P : (b + 1) * P, cols])

        def load_scales(h, ks):
            for k in ks:
                cols = slice(k * S + h * HALF, k * S + (h + 1) * HALF)
                nc.sync.dma_start(scales_all[:, cols], scales[0, cols].partition_broadcast(P))

        load_rows(logits[0], sparse_mask, 0, CHUNK)
        load_rows(dense[0], weight, 0, CHUNK)
        nc.sync.dma_start(offsets[:], offs)
        load_scales(0, range(K))
        load_rows(logits[1], sparse_mask, 1, S)
        load_scales(1, range(K - 1))
        load_rows(dense[1], weight, 1, S)
        load_scales(1, [K - 1])
        nc.sync.dma_start(row_gain[:], row_scale.rearrange("(b p) o -> p (b o)", p=P))

        identity = held.tile([P, P], F32, name="identity")
        make_identity(nc, identity[:])

        def make_sw(b, chunks_clamped_by_vector):
            gate = held.tile([P, S], F32, name=f"gate{b}")
            sw = held.tile([P, S], F32, name=f"sw{b}")
            chunks = [slice(c * CHUNK, (c + 1) * CHUNK) for c in range(S // CHUNK)]
            for c, cols in enumerate(chunks):
                nc.scalar.activation(gate[:, cols], logits[b][:, cols], ACT.Sigmoid)
                if c < chunks_clamped_by_vector:
                    nc.vector.tensor_scalar(gate[:, cols], gate[:, cols], 1.2, -0.1, ALU.mult, ALU.add)
                    nc.vector.tensor_scalar_max(gate[:, cols], gate[:, cols], 0.0)
                else:
                    nc.scalar.activation(gate[:, cols], gate[:, cols], ACT.Relu, bias=-0.1, scale=1.2)
            for cols in chunks:
                nc.vector.scalar_tensor_tensor(sw[:, cols], gate[:, cols], 1.0, dense[b][:, cols], ALU.min, ALU.mult)
            return sw

        def gather_term(sw, k, start, width, pieces=1):
            term = terms.tile([P, width], F32, name="term")
            step = width // pieces
            for within in range(0, width, step):
                first = k * S + start + within
                nc.vector.tensor_tensor(
                    term[:, within : within + step],
                    sw[:].indirect(offsets[:, first // 16 : (first + step) // 16]),
                    scales_all[:, first : first + step],
                    ALU.mult,
                )
            return term

        def scaled_sum(b, sw, ks, start, width, scaled, before_last=None):
            total = sums.tile([P, width], F32, name=f"total{b}_{start}")
            for k in ks:
                made = before_last() if before_last is not None and k == ks[-1] else None
                term = gather_term(sw, k, start, width)
                nc.tensor.matmul(total[:], identity[:], term[:], start=(k == ks[0]), stop=(k == ks[-1]))
            nc.scalar.activation(scaled, total[:], ACT.Identity, scale=row_gain[:, b : b + 1])
            return made

        def store(b, start, width, result):
            nc.sync.dma_start(out[b * P : (b + 1) * P, start : start + width], result[:])

        every_k = list(range(K))

        sw = make_sw(0, S // CHUNK - 1)
        scaled = held.tile([P, S], F32, name="scaled0")
        scaled_sum(0, sw, every_k, 0, HALF, scaled[:, 0:HALF])
        sw = scaled_sum(0, sw, every_k, HALF, HALF, scaled[:, HALF:S], before_last=lambda: make_sw(1, 0))
        store(0, 0, S, scaled)

        left = held.tile([P, HALF], F32, name="left")
        scaled_sum(1, sw, every_k, 0, HALF, left[:])
        store(1, 0, HALF, left)
        diagonal = held.tile([P, P], F32, name="diagonal")
        nc.scalar.activation(diagonal[:], identity[:], ACT.Identity, scale=row_gain[:, 1:2])
        columns = [slice(start, start + PIECE) for start in range(0, HALF, PIECE)]
        others = [sums.tile([P, PIECE], F32, name=f"others{cols.start}") for cols in columns]
        for k in every_k[:-1]:
            term = gather_term(sw, k, HALF, HALF, pieces=len(columns) if k == every_k[-2] else 1)
            for cols, total in zip(columns, others):
                nc.tensor.matmul(
                    total[:], diagonal[:], term[:, cols], start=(k == every_k[0]), stop=(k == every_k[-2])
                )
        term = gather_term(sw, every_k[-1], HALF, HALF, pieces=len(columns))
        for cols, total in zip(columns, others):
            result = held.tile([P, PIECE], F32, name=f"result{cols.start}")
            nc.vector.scalar_tensor_tensor(
                result[:], term[:, cols], row_gain[:, 1:2], total[:], ALU.mult, ALU.add
            )
            store(1, HALF + cols.start, PIECE, result)
